import numpy as np
import ml_dtypes


def mxq(x, axis, fmt="e4m3"):
    dtype, down = {"e4m3": (ml_dtypes.float8_e4m3fn, 7), "e5m2": (ml_dtypes.float8_e5m2, 14)}[fmt]
    v = np.moveaxis(np.asarray(x, np.float32).astype(ml_dtypes.bfloat16).astype(np.float64), axis, -1)
    blocks = v.reshape(v.shape[:-1] + (-1, 32))
    amax = np.abs(blocks).max(-1, keepdims=True)
    byte = np.maximum(np.where(amax > 0, np.frexp(amax)[1] - 1 + 127, 0) - down, 1)
    scale = np.exp2(byte - 127.0)
    codes = (blocks / scale).astype(np.float32).astype(dtype).astype(np.float64)
    return np.moveaxis((codes * scale).reshape(v.shape), -1, axis)


WIDE = False


def mx_kscale(k):
    if not WIDE:
        return np.ones(k)
    levels = np.array([30, -30])
    if k % 512:
        return np.exp2(np.random.permutation(np.resize(levels, k // 32))).repeat(32)
    a = np.empty((k // 512, 16))
    for p in range(k // 512):
        a[p, :8] = np.random.permutation(np.resize(levels, 8))
        for g in range(8):
            far = levels[np.abs(levels - a[p, g]) >= 10]
            a[p, g + 8] = far[np.random.randint(len(far))]
    return np.exp2(a.ravel()).repeat(32)


BF16 = ml_dtypes.bfloat16


def bf(x):
    return np.asarray(x, np.float32).astype(BF16)


def f64(x):
    return np.asarray(x).astype(np.float64)


B, CIN, COUT, E, G, NC = 2048, 512, 512, 4, 2, 2
OMEGA_0 = 30.0


def setup_inputs():
    s = mx_kscale(CIN)
    wb = np.sqrt(6.0 / CIN) / OMEGA_0
    return {"in_feats": bf(np.random.standard_normal((B, CIN)) * s),
            "tile_gate": bf(np.random.standard_normal((B, E)) / np.sqrt(E)),
            "W": bf(np.random.uniform(-wb, wb, (E, COUT, CIN)) / s)}


def reference(in_feats, tile_gate, W):
    xq = mxq(f64(in_feats), 1, "e5m2")
    wq = mxq(f64(W), 2, "e4m3")
    g = f64(tile_gate)
    out = np.zeros((B, COUT))
    for t in range(E):
        out = out + g[:, t:t + 1] * (xq @ wq[t].T)
    return np.sin(OMEGA_0 * out)

@@ -1,0 +1,216 @@
+import math
+from contextlib import ExitStack
+
+import concourse.mybir as mybir
+from concourse.masks import make_identity
+
+ROWS, CIN, COUT, EXPERTS = 2048, 512, 512, 4
+FLOPS = 2 * ROWS * CIN * COUT * EXPERTS
+
+F32 = mybir.dt.float32
+BF16 = mybir.dt.bfloat16
+U32 = mybir.dt.uint32
+I32 = mybir.dt.int32
+U8 = mybir.dt.uint8
+E5M2 = mybir.dt.float8_e5m2_x4
+E4M3 = mybir.dt.float8_e4m3fn_x4
+ALU = mybir.AluOpType
+ACT = mybir.ActivationFunctionType
+
+P = 128
+TILES = ROWS // P
+PAIRS = TILES // 2
+MAGIC = 12582912.0
+TURNS = 30.0 / (2.0 * math.pi)
+
+
+def tile_sinelayer_loe_pa_kernel(tc, in_feats, tile_gate, W, out):
+    nc = tc.nc
+    x_hbm = in_feats.rearrange("(p n) k -> p n k", n=TILES)
+    g_hbm = tile_gate.rearrange("(p n) e -> p (n e)", n=TILES)
+    o_hbm = out.rearrange("(p n) c -> p n c", n=TILES)
+
+    with ExitStack() as ctx:
+        keep = ctx.enter_context(tc.tile_pool(name="keep", bufs=1))
+        ring = ctx.enter_context(tc.tile_pool(name="ring", bufs=3))
+        psum = ctx.enter_context(tc.psum_pool(name="psum", bufs=8))
+        ctx.enter_context(tc.manual_schedule())
+
+        g_raw = keep.tile([P, TILES * EXPERTS], BF16, name="g_raw")
+        nc.scalar.dma_start(out=g_raw[:], in_=g_hbm)
+        warm = keep.tile([P, 1], F32, name="warm")
+        nc.vector.memset(warm[:], 0.0)
+        nc.scalar.activation(out=warm[:], in_=warm[:], func=ACT.Sin)
+        ident = keep.tile([P, P], F32, name="ident")
+        make_identity(nc, ident[:])
+        g32 = keep.tile([P, TILES * EXPERTS], F32, name="g32")
+
+        x_raw, w_raw = {}, {}
+
+        def load_x(u):
+            x_raw[u] = keep.tile([P, 2, CIN], BF16, name="x_raw%d" % u)
+            nc.sync.dma_start(out=x_raw[u][:], in_=x_hbm[:, 2 * u:2 * u + 2, :])
+
+        def load_w(t, b):
+            w_raw[t, b] = keep.tile([P, 2, CIN], BF16, name="w_raw%d_%d" % (t, b))
+            nc.sync.dma_start(out=w_raw[t, b][:], in_=W[t].rearrange("(p j) k -> p j k", j=4)[:, 2 * b:2 * b + 2, :])
+
+        bank = {}
+
+        def transposes(key, raw):
+            bank[key] = psum.tile([P, 512], F32, name="ps")
+            words = raw[:].rearrange("p s k -> p (s k)").bitcast(F32)
+            for s in range(2):
+                for e in range(2):
+                    nc.tensor.transpose(bank[key][:, (2 * s + e) * P:(2 * s + e + 1) * P],
+                                        words[:, 256 * s + e:256 * (s + 1):2], ident[:])
+
+        def copy_on(eng, dst, src):
+            if eng == "v":
+                nc.vector.tensor_copy(out=dst, in_=src)
+            else:
+                nc.scalar.copy(out=dst, in_=src)
+
+        xg, xc, xs, wg, wc, ws = {}, {}, {}, {}, {}, {}
+
+        def a_x(u, eng):
+            xg[u] = keep.tile([P, 1024], BF16, name="xg%d" % u, align_bytes=64)
+            copy_on(eng, xg[u][:].bitcast(F32).rearrange("q (s m e) -> q s m e", s=2, e=2),
+                    bank["x", u][:].rearrange("q (s e m) -> q s m e", s=2, e=2))
+
+        def q_x(u):
+            xc[u] = keep.tile([P, 256], U32, name="xc%d" % u, align_bytes=64)
+            xs[u] = keep.tile([P, 256], U8, name="xs%d" % u, align_bytes=64)
+            nc.vector.quantize_mx(out=xc[u][:].bitcast(E5M2), scales=xs[u][:], in_=xg[u][:])
+
+        def a_w(t, b, eng):
+            if b == 0:
+                wg[t] = keep.tile([P, 2048], BF16, name="wg%d" % t, align_bytes=64)
+            copy_on(eng, wg[t][:].bitcast(F32).rearrange("q (m b r) -> q m b r", b=2, r=4)[:, :, b, :],
+                    bank["w", t, b][:].rearrange("q (r m) -> q m r", r=4))
+
+        def q_w(t):
+            wc[t] = keep.tile([P, 512], U32, name="wc%d" % t, align_bytes=64)
+            ws[t] = keep.tile([P, 512], U8, name="ws%d" % t, align_bytes=64)
+            nc.vector.quantize_mx(out=wc[t][:].bitcast(E4M3), scales=ws[t][:], in_=wg[t][:])
+
+        def mm(u, t, s):
+            bank[u, t, s] = psum.tile([P, 512], F32, name="ps")
+            cols = slice(P * s, P * (s + 1))
+            nc.tensor.matmul_mx(out=bank[u, t, s][:], lhsT=xc[u][:, cols].bitcast(E5M2), lhsT_scale=xs[u][:, cols],
+                                rhs=wc[t][:].bitcast(E4M3), rhs_scale=ws[t][:], start=True, stop=True)
+
+        acc, ti, kf, fr, res = {}, {}, {}, {}, {}
+
+        def gcol(u, t, s):
+            c = (2 * u + s) * EXPERTS + t
+            return g32[:, c:c + 1]
+
+        def rd(u, t, s, eng="v"):
+            if t == 0 and s == 0:
+                acc[u] = ring.tile([P, 2, COUT], F32, name="acc", bufs=6)
+            if t == 0 and eng == "s":
+                nc.scalar.activation(out=acc[u][:, s, :], in_=bank[u, 0, s][:], func=ACT.Copy, scale=gcol(u, 0, s))
+            elif t == 0:
+                nc.vector.tensor_scalar(out=acc[u][:, s, :], in0=bank[u, 0, s][:], scalar1=gcol(u, 0, s), scalar2=None,
+                                        op0=ALU.mult)
+            else:
+                nc.vector.scalar_tensor_tensor(out=acc[u][:, s, :], in0=bank[u, t, s][:], scalar=gcol(u, t, s),
+                                               in1=acc[u][:, s, :], op0=ALU.mult, op1=ALU.add)
+
+        def sl(s):
+            return slice(0, 2) if s is None else slice(s, s + 1)
+
+        def d_g(u, s=None):
+            if s in (None, 0):
+                ti[u] = ring.tile([P, 2, COUT], I32, name="ti")
+            nc.gpsimd.tensor_scalar(out=ti[u][:, sl(s), :], in0=acc[u][:, sl(s), :], scalar1=MAGIC, scalar2=1.0,
+                                    op0=ALU.add, op1=ALU.mult)
+
+        def d_s(u, s=None):
+            if s in (None, 0):
+                ti[u] = ring.tile([P, 2, COUT], I32, name="ti")
+            nc.scalar.activation(out=ti[u][:, sl(s), :].bitcast(U32), in_=acc[u][:, sl(s), :], func=ACT.Copy, bias=MAGIC,
+                                 scale=1.0)
+
+        def cv(u, s=None):
+            if s in (None, 0):
+                kf[u] = ring.tile([P, 2, COUT], F32, name="kf")
+            nc.scalar.activation(out=kf[u][:, sl(s), :], in_=ti[u][:, sl(s), :].bitcast(U32), func=ACT.Copy, bias=-MAGIC,
+                                 scale=1.0)
+
+        def e_g(u, s=None):
+            if s in (None, 0):
+                fr[u] = ring.tile([P, 2, COUT], F32, name="fr")
+            nc.gpsimd.tensor_tensor(out=fr[u][:, sl(s), :], in0=kf[u][:, sl(s), :], in1=acc[u][:, sl(s), :], op=ALU.subtract)
+
+        def e_v(u, s=None):
+            if s in (None, 0):
+                fr[u] = ring.tile([P, 2, COUT], F32, name="fr")
+            nc.vector.scalar_tensor_tensor(out=fr[u][:, sl(s), :], in0=ti[u][:, sl(s), :], scalar=MAGIC,
+                                           in1=acc[u][:, sl(s), :], op0=ALU.subtract, op1=ALU.subtract)
+
+        def f_(u, s=None):
+            if s in (None, 0):
+                res[u] = ring.tile([P, 2, COUT], F32, name="res")
+            nc.scalar.activation(out=res[u][:, sl(s), :], in_=fr[u][:, sl(s), :], func=ACT.Sin, scale=-2.0 * math.pi)
+            nc.sync.dma_start(out=o_hbm[:, 2 * u:2 * u + 2, :][:, sl(s), :], in_=res[u][:, sl(s), :])
+
+        load_x(0)
+        for t in range(EXPERTS):
+            load_w(t, 0); load_w(t, 1)
+        for u in range(1, PAIRS):
+            load_x(u)
+        nc.vector.tensor_scalar(out=g32[:], in0=g_raw[:], scalar1=TURNS, scalar2=None, op0=ALU.mult)
+
+        def tx(u, eng="s"):
+            transposes(("x", u), x_raw[u]); a_x(u, eng)
+
+        def tw(t, b, eng="s"):
+            transposes(("w", t, b), w_raw[t, b]); a_w(t, b, eng)
+
+        def mm2(u, t):
+            mm(u, t, 0); mm(u, t, 1)
+
+        def rd2(u, t, eng="v"):
+            rd(u, t, 0, eng); rd(u, t, 1, eng)
+
+        tx(0, "v"); tw(0, 0); tw(0, 1, "v"); q_x(0); q_w(0)
+        tw(1, 0); tw(1, 1); q_w(1); tw(2, 0); tw(2, 1)
+        mm2(0, 0); rd2(0, 0); q_w(2)
+        tw(3, 0); tw(3, 1)
+        mm2(0, 1); rd2(0, 1); q_w(3)
+        tx(1); tx(2)
+        mm2(0, 2); rd2(0, 2); q_x(1)
+        tx(3); tx(4)
+        mm2(0, 3); rd2(0, 3)
+        d_g(0, 0); d_g(0, 1)
+        q_x(2)
+        mm2(1, 0); rd2(1, 0, "v")
+        tx(5); tx(6); tx(7)
+        q_x(3); q_x(4)
+
+        XQ = {1: (5, 6, 7)}
+        for u in range(1, PAIRS):
+            last = u == PAIRS - 1
+            mm2(u, 1); rd2(u, 1)
+            for v in XQ.get(u, ()):
+                q_x(v)
+            cv(u - 1, 0); e_g(u - 1, 0); cv(u - 1, 1); e_g(u - 1, 1)
+            if not last:
+                mm2(u + 1, 0); rd2(u + 1, 0, "s")
+            mm2(u, 2); rd2(u, 2)
+            f_(u - 1, 0)
+            mm2(u, 3); rd(u, 3, 0)
+            if not last:
+                d_g(u, 0)
+            else:
+                d_s(u, 0)
+            rd(u, 3, 1)
+            if not last:
+                d_g(u, 1)
+            else:
+                d_s(u, 1)
+            f_(u - 1, 1)
+        u = PAIRS - 1
+        e_v(u, 0); e_v(u, 1); f_(u, 0); f_(u, 1)

@@ -22,6 +22,7 @@ TILES = ROWS // P
 PAIRS = TILES // 2
 MAGIC = 12582912.0
 TURNS = 30.0 / (2.0 * math.pi)
+WARM0, WARM1 = 5, 2
 
 
 def tile_sinelayer_loe_pa_kernel(tc, in_feats, tile_gate, W, out):
@@ -161,6 +162,15 @@ def tile_sinelayer_loe_pa_kernel(tc, in_feats, tile_gate, W, out):
             load_w(t, 0); load_w(t, 1)
         for u in range(1, PAIRS):
             load_x(u)
+        zb = keep.tile([P, 512], BF16, name="zb")
+        nc.gpsimd.memset(zb[:], 0.0)
+
+        def warm(n):
+            for i in range(n):
+                junk = psum.tile([P, 512], F32, name="ps")
+                nc.tensor.matmul(out=junk[:], lhsT=zb[:, 0:P], rhs=zb[:], start=True, stop=True)
+
+        warm(WARM0)
         nc.vector.tensor_scalar(out=g32[:], in0=g_raw[:], scalar1=TURNS, scalar2=None, op0=ALU.mult)
 
         def tx(u, eng="s"):
@@ -176,30 +186,25 @@ def tile_sinelayer_loe_pa_kernel(tc, in_feats, tile_gate, W, out):
             rd(u, t, 0, eng); rd(u, t, 1, eng)
 
         tx(0, "v"); tw(0, 0); tw(0, 1, "v"); q_x(0); q_w(0)
-        tw(1, 0); tw(1, 1); q_w(1); tw(2, 0); tw(2, 1)
-        mm2(0, 0); rd2(0, 0); q_w(2)
-        tw(3, 0); tw(3, 1)
-        mm2(0, 1); rd2(0, 1); q_w(3)
-        tx(1); tx(2)
-        mm2(0, 2); rd2(0, 2); q_x(1)
-        tx(3); tx(4)
-        mm2(0, 3); rd2(0, 3)
-        d_g(0, 0); d_g(0, 1)
-        q_x(2)
-        mm2(1, 0); rd2(1, 0, "v")
-        tx(5); tx(6); tx(7)
-        q_x(3); q_x(4)
+        warm(WARM1)
+        tw(1, 0); tw(1, 1); tw(2, 0); q_w(1)
+        mm2(0, 0); rd2(0, 0, "v"); tw(2, 1); tw(3, 0); q_w(2)
+        mm2(0, 1); rd2(0, 1)
+        tw(3, 1); tx(1); q_w(3)
+        mm2(0, 2); rd2(0, 2)
+        tx(2); q_x(1)
+        mm2(0, 3); mm2(1, 0); rd(0, 3, 0); d_g(0, 0); rd(0, 3, 1); d_g(0, 1)
+        rd2(1, 0, "s"); q_x(2)
 
-        XQ = {1: (5, 6, 7)}
         for u in range(1, PAIRS):
             last = u == PAIRS - 1
             mm2(u, 1); rd2(u, 1)
-            for v in XQ.get(u, ()):
-                q_x(v)
             cv(u - 1, 0); e_g(u - 1, 0); cv(u - 1, 1); e_g(u - 1, 1)
             if not last:
                 mm2(u + 1, 0); rd2(u + 1, 0, "s")
             mm2(u, 2); rd2(u, 2)
+            if u + 2 < PAIRS:
+                tx(u + 2)
             f_(u - 1, 0)
             mm2(u, 3); rd(u, 3, 0)
             if not last:
@@ -211,6 +216,8 @@ def tile_sinelayer_loe_pa_kernel(tc, in_feats, tile_gate, W, out):
                 d_g(u, 1)
             else:
                 d_s(u, 1)
+            if u + 2 < PAIRS:
+                q_x(u + 2)
             f_(u - 1, 1)
         u = PAIRS - 1
         e_v(u, 0); e_v(u, 1); f_(u, 0); f_(u, 1)

@@ -22,7 +22,6 @@ TILES = ROWS // P
 PAIRS = TILES // 2
 MAGIC = 12582912.0
 TURNS = 30.0 / (2.0 * math.pi)
-WARM0, WARM1 = 5, 2
 
 
 def tile_sinelayer_loe_pa_kernel(tc, in_feats, tile_gate, W, out):
@@ -123,36 +122,36 @@ def tile_sinelayer_loe_pa_kernel(tc, in_feats, tile_gate, W, out):
             return slice(0, 2) if s is None else slice(s, s + 1)
 
         def d_g(u, s=None):
-            if s in (None, 0):
+            if u not in ti:
                 ti[u] = ring.tile([P, 2, COUT], I32, name="ti")
             nc.gpsimd.tensor_scalar(out=ti[u][:, sl(s), :], in0=acc[u][:, sl(s), :], scalar1=MAGIC, scalar2=1.0,
                                     op0=ALU.add, op1=ALU.mult)
 
         def d_s(u, s=None):
-            if s in (None, 0):
+            if u not in ti:
                 ti[u] = ring.tile([P, 2, COUT], I32, name="ti")
             nc.scalar.activation(out=ti[u][:, sl(s), :].bitcast(U32), in_=acc[u][:, sl(s), :], func=ACT.Copy, bias=MAGIC,
                                  scale=1.0)
 
         def cv(u, s=None):
-            if s in (None, 0):
+            if u not in kf:
                 kf[u] = ring.tile([P, 2, COUT], F32, name="kf")
             nc.scalar.activation(out=kf[u][:, sl(s), :], in_=ti[u][:, sl(s), :].bitcast(U32), func=ACT.Copy, bias=-MAGIC,
                                  scale=1.0)
 
         def e_g(u, s=None):
-            if s in (None, 0):
+            if u not in fr:
                 fr[u] = ring.tile([P, 2, COUT], F32, name="fr")
             nc.gpsimd.tensor_tensor(out=fr[u][:, sl(s), :], in0=kf[u][:, sl(s), :], in1=acc[u][:, sl(s), :], op=ALU.subtract)
 
         def e_v(u, s=None):
-            if s in (None, 0):
+            if u not in fr:
                 fr[u] = ring.tile([P, 2, COUT], F32, name="fr")
             nc.vector.scalar_tensor_tensor(out=fr[u][:, sl(s), :], in0=ti[u][:, sl(s), :], scalar=MAGIC,
                                            in1=acc[u][:, sl(s), :], op0=ALU.subtract, op1=ALU.subtract)
 
         def f_(u, s=None):
-            if s in (None, 0):
+            if u not in res:
                 res[u] = ring.tile([P, 2, COUT], F32, name="res")
             nc.scalar.activation(out=res[u][:, sl(s), :], in_=fr[u][:, sl(s), :], func=ACT.Sin, scale=-2.0 * math.pi)
             nc.sync.dma_start(out=o_hbm[:, 2 * u:2 * u + 2, :][:, sl(s), :], in_=res[u][:, sl(s), :])
@@ -162,15 +161,6 @@ def tile_sinelayer_loe_pa_kernel(tc, in_feats, tile_gate, W, out):
             load_w(t, 0); load_w(t, 1)
         for u in range(1, PAIRS):
             load_x(u)
-        zb = keep.tile([P, 512], BF16, name="zb")
-        nc.gpsimd.memset(zb[:], 0.0)
-
-        def warm(n):
-            for i in range(n):
-                junk = psum.tile([P, 512], F32, name="ps")
-                nc.tensor.matmul(out=junk[:], lhsT=zb[:, 0:P], rhs=zb[:], start=True, stop=True)
-
-        warm(WARM0)
         nc.vector.tensor_scalar(out=g32[:], in0=g_raw[:], scalar1=TURNS, scalar2=None, op0=ALU.mult)
 
         def tx(u, eng="s"):
@@ -186,38 +176,33 @@ def tile_sinelayer_loe_pa_kernel(tc, in_feats, tile_gate, W, out):
             rd(u, t, 0, eng); rd(u, t, 1, eng)
 
         tx(0, "v"); tw(0, 0); tw(0, 1, "v"); q_x(0); q_w(0)
-        warm(WARM1)
         tw(1, 0); tw(1, 1); tw(2, 0); q_w(1)
         mm2(0, 0); rd2(0, 0, "v"); tw(2, 1); tw(3, 0); q_w(2)
         mm2(0, 1); rd2(0, 1)
         tw(3, 1); tx(1); q_w(3)
         mm2(0, 2); rd2(0, 2)
         tx(2); q_x(1)
-        mm2(0, 3); mm2(1, 0); rd(0, 3, 0); d_g(0, 0); rd(0, 3, 1); d_g(0, 1)
+        mm2(0, 3); mm2(1, 0); rd(0, 3, 0); d_g(0, 0); rd(0, 3, 1)
         rd2(1, 0, "s"); q_x(2)
 
         for u in range(1, PAIRS):
             last = u == PAIRS - 1
             mm2(u, 1); rd2(u, 1)
-            cv(u - 1, 0); e_g(u - 1, 0); cv(u - 1, 1); e_g(u - 1, 1)
+            d_s(u - 1, 1); cv(u - 1, 0); e_v(u - 1, 1); e_g(u - 1, 0)
             if not last:
                 mm2(u + 1, 0); rd2(u + 1, 0, "s")
-            mm2(u, 2); rd2(u, 2)
             if u + 2 < PAIRS:
                 tx(u + 2)
-            f_(u - 1, 0)
-            mm2(u, 3); rd(u, 3, 0)
+            mm2(u, 2)
             if not last:
-                d_g(u, 0)
+                rd2(u, 2)
+                f_(u - 1, 1)
+                mm2(u, 3); rd(u, 3, 0); d_g(u, 0)
+                if u + 2 < PAIRS:
+                    q_x(u + 2)
+                rd(u, 3, 1)
+                f_(u - 1, 0)
             else:
-                d_s(u, 0)
-            rd(u, 3, 1)
-            if not last:
-                d_g(u, 1)
-            else:
-                d_s(u, 1)
-            if u + 2 < PAIRS:
-                q_x(u + 2)
-            f_(u - 1, 1)
-        u = PAIRS - 1
-        e_v(u, 0); e_v(u, 1); f_(u, 0); f_(u, 1)
+                mm2(u, 3)
+                rd(u, 2, 0); f_(u - 1, 1); rd(u, 2, 1); rd(u, 3, 0); d_s(u, 0); rd(u, 3, 1); f_(u - 1, 0); d_s(u, 1)
+                e_v(u, 0); f_(u, 0); e_v(u, 1); f_(u, 1)

@@ -175,15 +175,15 @@ def tile_sinelayer_loe_pa_kernel(tc, in_feats, tile_gate, W, out):
         def rd2(u, t, eng="v"):
             rd(u, t, 0, eng); rd(u, t, 1, eng)
 
-        tx(0, "v"); tw(0, 0); tw(0, 1, "v"); q_x(0); q_w(0)
-        tw(1, 0); tw(1, 1); tw(2, 0); q_w(1)
-        mm2(0, 0); rd2(0, 0, "v"); tw(2, 1); tw(3, 0); q_w(2)
+        tx(0, "v"); q_x(0); tw(0, 0); tw(0, 1, "v"); q_w(0)
+        tw(1, 0); tw(1, 1); tw(2, 0, "v"); q_w(1)
+        mm2(0, 0); tw(2, 1); rd(0, 0, 0, "s"); rd(0, 0, 1, "v"); tw(3, 0); q_w(2)
         mm2(0, 1); rd2(0, 1)
         tw(3, 1); tx(1); q_w(3)
-        mm2(0, 2); rd2(0, 2)
-        tx(2); q_x(1)
+        mm2(0, 2); q_x(1); rd2(0, 2)
+        tx(2); q_x(2)
         mm2(0, 3); mm2(1, 0); rd(0, 3, 0); d_g(0, 0); rd(0, 3, 1)
-        rd2(1, 0, "s"); q_x(2)
+        rd2(1, 0, "s")
 
         for u in range(1, PAIRS):
             last = u == PAIRS - 1
@@ -204,5 +204,5 @@ def tile_sinelayer_loe_pa_kernel(tc, in_feats, tile_gate, W, out):
                 f_(u - 1, 0)
             else:
                 mm2(u, 3)
-                rd(u, 2, 0); f_(u - 1, 1); rd(u, 2, 1); rd(u, 3, 0); d_s(u, 0); rd(u, 3, 1); f_(u - 1, 0); d_s(u, 1)
+                rd(u, 2, 0); f_(u - 1, 1); rd(u, 2, 1); rd(u, 3, 0); f_(u - 1, 0); d_s(u, 0); rd(u, 3, 1); d_s(u, 1)
                 e_v(u, 0); f_(u, 0); e_v(u, 1); f_(u, 1)

@@ -32,7 +32,7 @@ def tile_sinelayer_loe_pa_kernel(tc, in_feats, tile_gate, W, out):
 
     with ExitStack() as ctx:
         keep = ctx.enter_context(tc.tile_pool(name="keep", bufs=1))
-        ring = ctx.enter_context(tc.tile_pool(name="ring", bufs=3))
+        ring = ctx.enter_context(tc.tile_pool(name="ring", bufs=4))
         psum = ctx.enter_context(tc.psum_pool(name="psum", bufs=8))
         ctx.enter_context(tc.manual_schedule())
 
@@ -101,67 +101,61 @@ def tile_sinelayer_loe_pa_kernel(tc, in_feats, tile_gate, W, out):
                                 rhs=wc[t][:].bitcast(E4M3), rhs_scale=ws[t][:], start=True, stop=True)
 
         acc, ti, kf, fr, res = {}, {}, {}, {}, {}
+        WIDE = 2 * COUT
+        o_flat = out.rearrange("(p n) c -> p (n c)", n=TILES)
 
         def gcol(u, t, s):
             c = (2 * u + s) * EXPERTS + t
             return g32[:, c:c + 1]
 
+        def get(d, u, name, dt, bufs):
+            if u not in d:
+                d[u] = ring.tile([P, WIDE], dt, name=name, bufs=bufs)
+            return d[u]
+
         def rd(u, t, s, eng="v"):
-            if t == 0 and s == 0:
-                acc[u] = ring.tile([P, 2, COUT], F32, name="acc", bufs=6)
+            a = get(acc, u, "acc", F32, 6)[:, COUT * s:COUT * (s + 1)]
             if t == 0 and eng == "s":
-                nc.scalar.activation(out=acc[u][:, s, :], in_=bank[u, 0, s][:], func=ACT.Copy, scale=gcol(u, 0, s))
+                nc.scalar.activation(out=a, in_=bank[u, 0, s][:], func=ACT.Copy, scale=gcol(u, 0, s))
             elif t == 0:
-                nc.vector.tensor_scalar(out=acc[u][:, s, :], in0=bank[u, 0, s][:], scalar1=gcol(u, 0, s), scalar2=None,
-                                        op0=ALU.mult)
+                nc.vector.tensor_scalar(out=a, in0=bank[u, 0, s][:], scalar1=gcol(u, 0, s), scalar2=None, op0=ALU.mult)
             else:
-                nc.vector.scalar_tensor_tensor(out=acc[u][:, s, :], in0=bank[u, t, s][:], scalar=gcol(u, t, s),
-                                               in1=acc[u][:, s, :], op0=ALU.mult, op1=ALU.add)
+                nc.vector.scalar_tensor_tensor(out=a, in0=bank[u, t, s][:], scalar=gcol(u, t, s), in1=a, op0=ALU.mult, op1=ALU.add)
 
-        def sl(s):
-            return slice(0, 2) if s is None else slice(s, s + 1)
-
-        def d_g(u, s=None):
-            if u not in ti:
-                ti[u] = ring.tile([P, 2, COUT], I32, name="ti")
-            nc.gpsimd.tensor_scalar(out=ti[u][:, sl(s), :], in0=acc[u][:, sl(s), :], scalar1=MAGIC, scalar2=1.0,
+        def round_g(u, lo, hi):
+            nc.gpsimd.tensor_scalar(out=get(ti, u, "ti", I32, 4)[:, lo:hi], in0=acc[u][:, lo:hi], scalar1=MAGIC, scalar2=1.0,
                                     op0=ALU.add, op1=ALU.mult)
 
-        def d_s(u, s=None):
-            if u not in ti:
-                ti[u] = ring.tile([P, 2, COUT], I32, name="ti")
-            nc.scalar.activation(out=ti[u][:, sl(s), :].bitcast(U32), in_=acc[u][:, sl(s), :], func=ACT.Copy, bias=MAGIC,
-                                 scale=1.0)
+        def round_s(u, lo, hi):
+            nc.scalar.activation(out=get(ti, u, "ti", I32, 4)[:, lo:hi].bitcast(U32), in_=acc[u][:, lo:hi], func=ACT.Copy,
+                                 bias=MAGIC, scale=1.0)
 
-        def cv(u, s=None):
-            if u not in kf:
-                kf[u] = ring.tile([P, 2, COUT], F32, name="kf")
-            nc.scalar.activation(out=kf[u][:, sl(s), :], in_=ti[u][:, sl(s), :].bitcast(U32), func=ACT.Copy, bias=-MAGIC,
-                                 scale=1.0)
+        def to_float(u, lo, hi):
+            nc.scalar.activation(out=get(kf, u, "kf", F32, 4)[:, lo:hi], in_=ti[u][:, lo:hi].bitcast(U32), func=ACT.Copy,
+                                 bias=-MAGIC, scale=1.0)
 
-        def e_g(u, s=None):
-            if u not in fr:
-                fr[u] = ring.tile([P, 2, COUT], F32, name="fr")
-            nc.gpsimd.tensor_tensor(out=fr[u][:, sl(s), :], in0=kf[u][:, sl(s), :], in1=acc[u][:, sl(s), :], op=ALU.subtract)
+        def sub_g(u, lo, hi):
+            nc.gpsimd.tensor_tensor(out=get(fr, u, "fr", F32, 4)[:, lo:hi], in0=kf[u][:, lo:hi], in1=acc[u][:, lo:hi],
+                                    op=ALU.subtract)
 
-        def e_v(u, s=None):
-            if u not in fr:
-                fr[u] = ring.tile([P, 2, COUT], F32, name="fr")
-            nc.vector.scalar_tensor_tensor(out=fr[u][:, sl(s), :], in0=ti[u][:, sl(s), :], scalar=MAGIC,
-                                           in1=acc[u][:, sl(s), :], op0=ALU.subtract, op1=ALU.subtract)
+        def sub_v(u, lo, hi):
+            nc.vector.scalar_tensor_tensor(out=get(fr, u, "fr", F32, 4)[:, lo:hi], in0=ti[u][:, lo:hi], scalar=MAGIC,
+                                           in1=acc[u][:, lo:hi], op0=ALU.subtract, op1=ALU.subtract)
 
-        def f_(u, s=None):
-            if u not in res:
-                res[u] = ring.tile([P, 2, COUT], F32, name="res")
-            nc.scalar.activation(out=res[u][:, sl(s), :], in_=fr[u][:, sl(s), :], func=ACT.Sin, scale=-2.0 * math.pi)
-            nc.sync.dma_start(out=o_hbm[:, 2 * u:2 * u + 2, :][:, sl(s), :], in_=res[u][:, sl(s), :])
+        def sine(u, lo, hi):
+            nc.scalar.activation(out=get(res, u, "res", F32, 4)[:, lo:hi], in_=fr[u][:, lo:hi], func=ACT.Sin, scale=-2.0 * math.pi)
+            nc.sync.dma_start(out=o_flat[:, WIDE * u + lo:WIDE * u + hi], in_=res[u][:, lo:hi])
 
-        load_x(0)
-        for t in range(EXPERTS):
-            load_w(t, 0); load_w(t, 1)
-        for u in range(1, PAIRS):
-            load_x(u)
-        nc.vector.tensor_scalar(out=g32[:], in0=g_raw[:], scalar1=TURNS, scalar2=None, op0=ALU.mult)
+        def D_G(u, k): round_g(u, 0, 128 * k)
+        def D_S(u, k): round_s(u, 128 * k, WIDE)
+        def CV(u, k): to_float(u, 0, 128 * k)
+        def E_G(u, k): sub_g(u, 0, 128 * k)
+        def E_V(u, k): sub_v(u, 128 * k, WIDE)
+        def SIN_G(u, k): sine(u, 0, 128 * k)
+        def SIN_V(u, k): sine(u, 128 * k, WIDE)
+        def d_s(u, s): round_s(u, COUT * s, COUT * (s + 1))
+        def e_v(u, s): sub_v(u, COUT * s, COUT * (s + 1))
+        def f_(u, s): sine(u, COUT * s, COUT * (s + 1))
 
         def tx(u, eng="s"):
             transposes(("x", u), x_raw[u]); a_x(u, eng)
@@ -175,6 +169,14 @@ def tile_sinelayer_loe_pa_kernel(tc, in_feats, tile_gate, W, out):
         def rd2(u, t, eng="v"):
             rd(u, t, 0, eng); rd(u, t, 1, eng)
 
+        K = [6] * 6 + [3, 0]
+        load_x(0)
+        for t in range(EXPERTS):
+            load_w(t, 0); load_w(t, 1)
+        for u in range(1, PAIRS):
+            load_x(u)
+        nc.vector.tensor_scalar(out=g32[:], in0=g_raw[:], scalar1=TURNS, scalar2=None, op0=ALU.mult)
+
         tx(0, "v"); q_x(0); tw(0, 0); tw(0, 1, "v"); q_w(0)
         tw(1, 0); tw(1, 1); tw(2, 0, "v"); q_w(1)
         mm2(0, 0); tw(2, 1); rd(0, 0, 0, "s"); rd(0, 0, 1, "v"); tw(3, 0); q_w(2)
@@ -182,27 +184,32 @@ def tile_sinelayer_loe_pa_kernel(tc, in_feats, tile_gate, W, out):
         tw(3, 1); tx(1); q_w(3)
         mm2(0, 2); q_x(1); rd2(0, 2)
         tx(2); q_x(2)
-        mm2(0, 3); mm2(1, 0); rd(0, 3, 0); d_g(0, 0); rd(0, 3, 1)
-        rd2(1, 0, "s")
+        mm2(0, 3); mm2(1, 0); rd(0, 3, 0); rd(0, 3, 1)
+        rd2(1, 0, "s"); tx(3)
 
-        for u in range(1, PAIRS):
-            last = u == PAIRS - 1
-            mm2(u, 1); rd2(u, 1)
-            d_s(u - 1, 1); cv(u - 1, 0); e_v(u - 1, 1); e_g(u - 1, 0)
-            if not last:
-                mm2(u + 1, 0); rd2(u + 1, 0, "s")
-            if u + 2 < PAIRS:
-                tx(u + 2)
-            mm2(u, 2)
-            if not last:
-                rd2(u, 2)
-                f_(u - 1, 1)
-                mm2(u, 3); rd(u, 3, 0); d_g(u, 0)
-                if u + 2 < PAIRS:
-                    q_x(u + 2)
-                rd(u, 3, 1)
-                f_(u - 1, 0)
-            else:
-                mm2(u, 3)
-                rd(u, 2, 0); f_(u - 1, 1); rd(u, 2, 1); rd(u, 3, 0); f_(u - 1, 0); d_s(u, 0); rd(u, 3, 1); d_s(u, 1)
-                e_v(u, 0); f_(u, 0); e_v(u, 1); f_(u, 1)
+        def period(p):
+            k1 = K[p - 1]; k2 = K[p - 2] if p >= 2 else 0
+            mm2(p, 1)
+            D_G(p - 1, k1); D_S(p - 1, k1)
+            rd2(p, 1)
+            if p + 1 < PAIRS:
+                mm2(p + 1, 0); rd(p + 1, 0, 0, "s")
+            CV(p - 1, k1); E_G(p - 1, k1)
+            E_V(p - 1, k1)
+            if p + 2 < PAIRS:
+                q_x(p + 2)
+            mm2(p, 2)
+            if p >= 2: SIN_G(p - 2, k2)
+            if p + 1 < PAIRS:
+                rd(p + 1, 0, 1, "s")
+            if p + 3 < PAIRS:
+                tx(p + 3)
+            rd2(p, 2)
+            mm2(p, 3)
+            if p < PAIRS - 1:
+                rd2(p, 3)
+                SIN_V(p - 1, k1)
+        for p in range(1, PAIRS):
+            period(p)
+        p = PAIRS - 1
+        SIN_V(p - 1, K[p - 1]); rd(p, 3, 0); SIN_G(p - 1, K[p - 1]); d_s(p, 0); rd(p, 3, 1); d_s(p, 1); e_v(p, 0); e_v(p, 1); f_(p, 0); f_(p, 1)

@@ -101,6 +101,7 @@ def tile_sinelayer_loe_pa_kernel(tc, in_feats, tile_gate, W, out):
                                 rhs=wc[t][:].bitcast(E4M3), rhs_scale=ws[t][:], start=True, stop=True)
 
         acc, ti, kf, fr, res = {}, {}, {}, {}, {}
+        UNIT = 64
         WIDE = 2 * COUT
         o_flat = out.rearrange("(p n) c -> p (n c)", n=TILES)
 
@@ -146,13 +147,13 @@ def tile_sinelayer_loe_pa_kernel(tc, in_feats, tile_gate, W, out):
             nc.scalar.activation(out=get(res, u, "res", F32, 4)[:, lo:hi], in_=fr[u][:, lo:hi], func=ACT.Sin, scale=-2.0 * math.pi)
             nc.sync.dma_start(out=o_flat[:, WIDE * u + lo:WIDE * u + hi], in_=res[u][:, lo:hi])
 
-        def D_G(u, k): round_g(u, 0, 128 * k)
-        def D_S(u, k): round_s(u, 128 * k, WIDE)
-        def CV(u, k): to_float(u, 0, 128 * k)
-        def E_G(u, k): sub_g(u, 0, 128 * k)
-        def E_V(u, k): sub_v(u, 128 * k, WIDE)
-        def SIN_G(u, k): sine(u, 0, 128 * k)
-        def SIN_V(u, k): sine(u, 128 * k, WIDE)
+        def D_G(u, k): round_g(u, 0, UNIT * k)
+        def D_S(u, k): round_s(u, UNIT * k, WIDE)
+        def CV(u, k): to_float(u, 0, UNIT * k)
+        def E_G(u, k): sub_g(u, 0, UNIT * k)
+        def E_V(u, k): sub_v(u, UNIT * k, WIDE)
+        def SIN_G(u, k): sine(u, 0, UNIT * k)
+        def SIN_V(u, k): sine(u, UNIT * k, WIDE)
         def d_s(u, s): round_s(u, COUT * s, COUT * (s + 1))
         def e_v(u, s): sub_v(u, COUT * s, COUT * (s + 1))
         def f_(u, s): sine(u, COUT * s, COUT * (s + 1))
@@ -169,7 +170,7 @@ def tile_sinelayer_loe_pa_kernel(tc, in_feats, tile_gate, W, out):
         def rd2(u, t, eng="v"):
             rd(u, t, 0, eng); rd(u, t, 1, eng)
 
-        K = [6] * 6 + [3, 0]
+        K = [11] * 6 + [6, 0]
         load_x(0)
         for t in range(EXPERTS):
             load_w(t, 0); load_w(t, 1)

@@ -196,16 +196,17 @@ def tile_sinelayer_loe_pa_kernel(tc, in_feats, tile_gate, W, out):
             if p + 1 < PAIRS:
                 mm2(p + 1, 0); rd(p + 1, 0, 0, "s")
             CV(p - 1, k1); E_G(p - 1, k1)
+            mm2(p, 2)
+            rd(p, 2, 0)
             E_V(p - 1, k1)
             if p + 2 < PAIRS:
                 q_x(p + 2)
-            mm2(p, 2)
             if p >= 2: SIN_G(p - 2, k2)
             if p + 1 < PAIRS:
                 rd(p + 1, 0, 1, "s")
             if p + 3 < PAIRS:
                 tx(p + 3)
-            rd2(p, 2)
+            rd(p, 2, 1)
             mm2(p, 3)
             if p < PAIRS - 1:
                 rd2(p, 3)

@@ -20,8 +20,10 @@ ACT = mybir.ActivationFunctionType
 P = 128
 TILES = ROWS // P
 PAIRS = TILES // 2
-MAGIC = 12582912.0
-TURNS = 30.0 / (2.0 * math.pi)
+STEP = 128.0
+BIAS = 1614807040.0
+FBIAS = 1.5 * 2.0 ** 65
+TURNS = STEP * 30.0 / (2.0 * math.pi)
 
 
 def tile_sinelayer_loe_pa_kernel(tc, in_feats, tile_gate, W, out):
@@ -114,6 +116,10 @@ def tile_sinelayer_loe_pa_kernel(tc, in_feats, tile_gate, W, out):
                 d[u] = ring.tile([P, WIDE], dt, name=name, bufs=bufs)
             return d[u]
 
+        def rd_part(u, t, s, lo, hi):
+            a = acc[u][:, COUT * s + lo:COUT * s + hi]
+            nc.vector.scalar_tensor_tensor(out=a, in0=bank[u, t, s][:, lo:hi], scalar=gcol(u, t, s), in1=a, op0=ALU.mult, op1=ALU.add)
+
         def rd(u, t, s, eng="v"):
             a = get(acc, u, "acc", F32, 6)[:, COUT * s:COUT * (s + 1)]
             if t == 0 and eng == "s":
@@ -123,37 +129,34 @@ def tile_sinelayer_loe_pa_kernel(tc, in_feats, tile_gate, W, out):
             else:
                 nc.vector.scalar_tensor_tensor(out=a, in0=bank[u, t, s][:], scalar=gcol(u, t, s), in1=a, op0=ALU.mult, op1=ALU.add)
 
-        def round_g(u, lo, hi):
-            nc.gpsimd.tensor_scalar(out=get(ti, u, "ti", I32, 4)[:, lo:hi], in0=acc[u][:, lo:hi], scalar1=MAGIC, scalar2=1.0,
-                                    op0=ALU.add, op1=ALU.mult)
-
         def round_s(u, lo, hi):
             nc.scalar.activation(out=get(ti, u, "ti", I32, 4)[:, lo:hi].bitcast(U32), in_=acc[u][:, lo:hi], func=ACT.Copy,
-                                 bias=MAGIC, scale=1.0)
+                                 bias=BIAS, scale=1.0)
 
-        def to_float(u, lo, hi):
-            nc.scalar.activation(out=get(kf, u, "kf", F32, 4)[:, lo:hi], in_=ti[u][:, lo:hi].bitcast(U32), func=ACT.Copy,
-                                 bias=-MAGIC, scale=1.0)
+        def round_v(u, lo, hi):
+            nc.vector.tensor_scalar(out=get(ti, u, "ti", I32, 4)[:, lo:hi], in0=acc[u][:, lo:hi], scalar1=BIAS, scalar2=None, op0=ALU.add)
+
+        def cvt_g(u, lo, hi):
+            nc.gpsimd.tensor_scalar(out=get(kf, u, "kf", F32, 4)[:, lo:hi], in0=ti[u][:, lo:hi].bitcast(F32), scalar1=-FBIAS,
+                                    scalar2=2.0 ** -42, op0=ALU.add, op1=ALU.mult)
 
         def sub_g(u, lo, hi):
             nc.gpsimd.tensor_tensor(out=get(fr, u, "fr", F32, 4)[:, lo:hi], in0=kf[u][:, lo:hi], in1=acc[u][:, lo:hi],
                                     op=ALU.subtract)
 
         def sub_v(u, lo, hi):
-            nc.vector.scalar_tensor_tensor(out=get(fr, u, "fr", F32, 4)[:, lo:hi], in0=ti[u][:, lo:hi], scalar=MAGIC,
+            nc.vector.scalar_tensor_tensor(out=get(fr, u, "fr", F32, 4)[:, lo:hi], in0=ti[u][:, lo:hi], scalar=BIAS,
                                            in1=acc[u][:, lo:hi], op0=ALU.subtract, op1=ALU.subtract)
 
         def sine(u, lo, hi):
-            nc.scalar.activation(out=get(res, u, "res", F32, 4)[:, lo:hi], in_=fr[u][:, lo:hi], func=ACT.Sin, scale=-2.0 * math.pi)
+            nc.scalar.activation(out=get(res, u, "res", F32, 4)[:, lo:hi], in_=fr[u][:, lo:hi], func=ACT.Sin, scale=-2.0 * math.pi / STEP)
             nc.sync.dma_start(out=o_flat[:, WIDE * u + lo:WIDE * u + hi], in_=res[u][:, lo:hi])
 
-        def D_G(u, k): round_g(u, 0, UNIT * k)
-        def D_S(u, k): round_s(u, UNIT * k, WIDE)
-        def CV(u, k): to_float(u, 0, UNIT * k)
-        def E_G(u, k): sub_g(u, 0, UNIT * k)
-        def E_V(u, k): sub_v(u, UNIT * k, WIDE)
-        def SIN_G(u, k): sine(u, 0, UNIT * k)
-        def SIN_V(u, k): sine(u, UNIT * k, WIDE)
+        def C_G(u, k): cvt_g(u, WIDE - UNIT * k, WIDE)
+        def E_G(u, k): sub_g(u, WIDE - UNIT * k, WIDE)
+        def E_V(u, k): sub_v(u, 0, WIDE - UNIT * k)
+        def SIN_G(u, k): sine(u, WIDE - UNIT * k, WIDE)
+        def SIN_V(u, k): sine(u, 0, WIDE - UNIT * k)
         def d_s(u, s): round_s(u, COUT * s, COUT * (s + 1))
         def e_v(u, s): sub_v(u, COUT * s, COUT * (s + 1))
         def f_(u, s): sine(u, COUT * s, COUT * (s + 1))
@@ -170,7 +173,7 @@ def tile_sinelayer_loe_pa_kernel(tc, in_feats, tile_gate, W, out):
         def rd2(u, t, eng="v"):
             rd(u, t, 0, eng); rd(u, t, 1, eng)
 
-        K = [11] * 6 + [6, 0]
+        K = [13] * 6 + [9, 3]
         load_x(0)
         for t in range(EXPERTS):
             load_w(t, 0); load_w(t, 1)
@@ -186,21 +189,22 @@ def tile_sinelayer_loe_pa_kernel(tc, in_feats, tile_gate, W, out):
         mm2(0, 2); q_x(1); rd2(0, 2)
         tx(2); q_x(2)
         mm2(0, 3); mm2(1, 0); rd(0, 3, 0); rd(0, 3, 1)
-        rd2(1, 0, "s"); tx(3)
+        rd2(1, 0, "s"); tx(3); d_s(0, 0)
 
         def period(p):
             k1 = K[p - 1]; k2 = K[p - 2] if p >= 2 else 0
             mm2(p, 1)
-            D_G(p - 1, k1); D_S(p - 1, k1)
-            rd2(p, 1)
-            if p + 1 < PAIRS:
-                mm2(p + 1, 0); rd(p + 1, 0, 0, "s")
-            CV(p - 1, k1); E_G(p - 1, k1)
-            mm2(p, 2)
-            rd(p, 2, 0)
-            E_V(p - 1, k1)
+            d_s(p - 1, 1)
+            rd(p, 1, 0)
             if p + 2 < PAIRS:
                 q_x(p + 2)
+            E_V(p - 1, k1)
+            C_G(p - 1, k1); E_G(p - 1, k1)
+            rd(p, 1, 1)
+            if p + 1 < PAIRS:
+                mm2(p + 1, 0); rd(p + 1, 0, 0, "s")
+            mm2(p, 2)
+            rd(p, 2, 0)
             if p >= 2: SIN_G(p - 2, k2)
             if p + 1 < PAIRS:
                 rd(p + 1, 0, 1, "s")
@@ -208,10 +212,20 @@ def tile_sinelayer_loe_pa_kernel(tc, in_feats, tile_gate, W, out):
                 tx(p + 3)
             rd(p, 2, 1)
             mm2(p, 3)
+            SIN_V(p - 1, k1)
+            rd(p, 3, 0); d_s(p, 0)
             if p < PAIRS - 1:
-                rd2(p, 3)
-                SIN_V(p - 1, k1)
-        for p in range(1, PAIRS):
+                rd(p, 3, 1)
+        for p in range(1, PAIRS - 1):
             period(p)
         p = PAIRS - 1
-        SIN_V(p - 1, K[p - 1]); rd(p, 3, 0); SIN_G(p - 1, K[p - 1]); d_s(p, 0); rd(p, 3, 1); d_s(p, 1); e_v(p, 0); e_v(p, 1); f_(p, 0); f_(p, 1)
+        H = COUT // 2
+        mm2(p, 1); d_s(p - 1, 1); rd(p, 1, 0); E_V(p - 1, K[p - 1]); C_G(p - 1, K[p - 1]); E_G(p - 1, K[p - 1])
+        mm2(p, 2); SIN_G(p - 2, K[p - 2]); rd(p, 2, 0); mm2(p, 3); rd(p, 3, 0); SIN_V(p - 1, K[p - 1]); d_s(p, 0)
+        G7 = COUT - UNIT * K[p]
+        cvt_g(p, G7, COUT); sub_g(p, G7, COUT)
+        rd(p, 1, 1); rd(p, 2, 1); sub_v(p, 0, G7); SIN_G(p - 1, K[p - 1]); sine(p, 0, G7)
+        rd_part(p, 3, 1, 0, H); rd_part(p, 3, 1, H, COUT)
+        round_v(p, COUT, COUT + H); round_v(p, COUT + H, WIDE)
+        sub_v(p, COUT, COUT + H); sub_v(p, COUT + H, WIDE)
+        sine(p, G7, COUT); sine(p, COUT, COUT + H); sine(p, COUT + H, WIDE)

@@ -183,13 +183,13 @@ def tile_sinelayer_loe_pa_kernel(tc, in_feats, tile_gate, W, out):
 
         tx(0, "v"); q_x(0); tw(0, 0); tw(0, 1, "v"); q_w(0)
         tw(1, 0); tw(1, 1); tw(2, 0, "v"); q_w(1)
-        mm2(0, 0); tw(2, 1); rd(0, 0, 0, "s"); rd(0, 0, 1, "v"); tw(3, 0); q_w(2)
+        tw(2, 1); mm2(0, 0); rd(0, 0, 0, "s"); rd(0, 0, 1, "v"); tw(3, 0); q_w(2); tw(3, 1)
         mm2(0, 1); rd2(0, 1)
-        tw(3, 1); tx(1); q_w(3)
+        tx(1); q_w(3)
         mm2(0, 2); q_x(1); rd2(0, 2)
-        tx(2); q_x(2)
+        tx(2); tx(3); q_x(2)
         mm2(0, 3); mm2(1, 0); rd(0, 3, 0); rd(0, 3, 1)
-        rd2(1, 0, "s"); tx(3); d_s(0, 0)
+        rd2(1, 0, "s"); d_s(0, 0)
 
         def period(p):
             k1 = K[p - 1]; k2 = K[p - 2] if p >= 2 else 0

@@ -205,14 +205,13 @@ def tile_sinelayer_loe_pa_kernel(tc, in_feats, tile_gate, W, out):
                 mm2(p + 1, 0); rd(p + 1, 0, 0, "s")
             mm2(p, 2)
             rd(p, 2, 0)
-            if p >= 2: SIN_G(p - 2, k2)
+            if p >= 2: sine(p - 2, 0, WIDE)
             if p + 1 < PAIRS:
                 rd(p + 1, 0, 1, "s")
             if p + 3 < PAIRS:
                 tx(p + 3)
             rd(p, 2, 1)
             mm2(p, 3)
-            SIN_V(p - 1, k1)
             rd(p, 3, 0); d_s(p, 0)
             if p < PAIRS - 1:
                 rd(p, 3, 1)
@@ -221,7 +220,7 @@ def tile_sinelayer_loe_pa_kernel(tc, in_feats, tile_gate, W, out):
         p = PAIRS - 1
         H = COUT // 2
         mm2(p, 1); d_s(p - 1, 1); rd(p, 1, 0); E_V(p - 1, K[p - 1]); C_G(p - 1, K[p - 1]); E_G(p - 1, K[p - 1])
-        mm2(p, 2); SIN_G(p - 2, K[p - 2]); rd(p, 2, 0); mm2(p, 3); rd(p, 3, 0); SIN_V(p - 1, K[p - 1]); d_s(p, 0)
+        mm2(p, 2); sine(p - 2, 0, WIDE); rd(p, 2, 0); mm2(p, 3); rd(p, 3, 0); SIN_V(p - 1, K[p - 1]); d_s(p, 0)
         G7 = COUT - UNIT * K[p]
         cvt_g(p, G7, COUT); sub_g(p, G7, COUT)
         rd(p, 1, 1); rd(p, 2, 1); sub_v(p, 0, G7); SIN_G(p - 1, K[p - 1]); sine(p, 0, G7)

@@ -46,6 +46,8 @@ def tile_sinelayer_loe_pa_kernel(tc, in_feats, tile_gate, W, out):
         ident = keep.tile([P, P], F32, name="ident")
         make_identity(nc, ident[:])
         g32 = keep.tile([P, TILES * EXPERTS], F32, name="g32")
+        neg_ident = keep.tile([P, P], F32, name="neg_ident")
+        nc.gpsimd.tensor_scalar(out=neg_ident[:], in0=ident[:], scalar1=-1.0, scalar2=0.0, op0=ALU.mult, op1=ALU.add)
 
         x_raw, w_raw = {}, {}
 
@@ -153,6 +155,20 @@ def tile_sinelayer_loe_pa_kernel(tc, in_feats, tile_gate, W, out):
             nc.sync.dma_start(out=o_flat[:, WIDE * u + lo:WIDE * u + hi], in_=res[u][:, lo:hi])
 
         def C_G(u, k): cvt_g(u, WIDE - UNIT * k, WIDE)
+
+        def C_ALL(u): cvt_g(u, 0, WIDE)
+
+        def E_PE(u, k):
+            v = WIDE - UNIT * k
+            bank["e", u] = psum.tile([P, 512], F32, name="ps")
+            nc.tensor.matmul(out=bank["e", u][:, 0:v], lhsT=ident[:], rhs=kf[u][:, 0:v], start=True, stop=False)
+            nc.tensor.matmul(out=bank["e", u][:, 0:v], lhsT=neg_ident[:], rhs=acc[u][:, 0:v], start=False, stop=True)
+
+        def sine_pair(u, k):
+            v = WIDE - UNIT * k
+            nc.scalar.activation(out=get(res, u, "res", F32, 4)[:, 0:v], in_=bank["e", u][:, 0:v], func=ACT.Sin, scale=-2.0 * math.pi / STEP)
+            nc.scalar.activation(out=res[u][:, v:WIDE], in_=fr[u][:, v:WIDE], func=ACT.Sin, scale=-2.0 * math.pi / STEP)
+            nc.sync.dma_start(out=o_flat[:, WIDE * u:WIDE * (u + 1)], in_=res[u][:])
         def E_G(u, k): sub_g(u, WIDE - UNIT * k, WIDE)
         def E_V(u, k): sub_v(u, 0, WIDE - UNIT * k)
         def SIN_G(u, k): sine(u, WIDE - UNIT * k, WIDE)
@@ -194,18 +210,18 @@ def tile_sinelayer_loe_pa_kernel(tc, in_feats, tile_gate, W, out):
         def period(p):
             k1 = K[p - 1]; k2 = K[p - 2] if p >= 2 else 0
             mm2(p, 1)
+            if p >= 2: E_PE(p - 2, k2)
             d_s(p - 1, 1)
             rd(p, 1, 0)
             if p + 2 < PAIRS:
                 q_x(p + 2)
-            E_V(p - 1, k1)
-            C_G(p - 1, k1); E_G(p - 1, k1)
+            C_ALL(p - 1); E_G(p - 1, k1)
             rd(p, 1, 1)
             if p + 1 < PAIRS:
                 mm2(p + 1, 0); rd(p + 1, 0, 0, "s")
             mm2(p, 2)
             rd(p, 2, 0)
-            if p >= 2: sine(p - 2, 0, WIDE)
+            if p >= 2: sine_pair(p - 2, k2)
             if p + 1 < PAIRS:
                 rd(p + 1, 0, 1, "s")
             if p + 3 < PAIRS:
@@ -219,8 +235,8 @@ def tile_sinelayer_loe_pa_kernel(tc, in_feats, tile_gate, W, out):
             period(p)
         p = PAIRS - 1
         H = COUT // 2
-        mm2(p, 1); d_s(p - 1, 1); rd(p, 1, 0); E_V(p - 1, K[p - 1]); C_G(p - 1, K[p - 1]); E_G(p - 1, K[p - 1])
-        mm2(p, 2); sine(p - 2, 0, WIDE); rd(p, 2, 0); mm2(p, 3); rd(p, 3, 0); SIN_V(p - 1, K[p - 1]); d_s(p, 0)
+        mm2(p, 1); E_PE(p - 2, K[p - 2]); d_s(p - 1, 1); rd(p, 1, 0); E_V(p - 1, K[p - 1]); C_G(p - 1, K[p - 1]); E_G(p - 1, K[p - 1])
+        mm2(p, 2); sine_pair(p - 2, K[p - 2]); rd(p, 2, 0); mm2(p, 3); rd(p, 3, 0); SIN_V(p - 1, K[p - 1]); d_s(p, 0)
         G7 = COUT - UNIT * K[p]
         cvt_g(p, G7, COUT); sub_g(p, G7, COUT)
         rd(p, 1, 1); rd(p, 2, 1); sub_v(p, 0, G7); SIN_G(p - 1, K[p - 1]); sine(p, 0, G7)

@@ -48,6 +48,12 @@ def tile_sinelayer_loe_pa_kernel(tc, in_feats, tile_gate, W, out):
         g32 = keep.tile([P, TILES * EXPERTS], F32, name="g32")
         neg_ident = keep.tile([P, P], F32, name="neg_ident")
         nc.gpsimd.tensor_scalar(out=neg_ident[:], in0=ident[:], scalar1=-1.0, scalar2=0.0, op0=ALU.mult, op1=ALU.add)
+        small_ident = keep.tile([P, P], F32, name="small_ident")
+        nc.gpsimd.tensor_scalar(out=small_ident[:], in0=ident[:], scalar1=2.0 ** -42, scalar2=0.0, op0=ALU.mult, op1=ALU.add)
+        big_ident = keep.tile([P, P], BF16, name="big_ident")
+        nc.gpsimd.tensor_scalar(out=big_ident[:], in0=ident[:], scalar1=-1.5 * 2.0 ** 23, scalar2=0.0, op0=ALU.mult, op1=ALU.add)
+        ones = keep.tile([P, 512], BF16, name="ones")
+        nc.gpsimd.memset(ones[:], 1.0)
 
         x_raw, w_raw = {}, {}
 
@@ -161,7 +167,8 @@ def tile_sinelayer_loe_pa_kernel(tc, in_feats, tile_gate, W, out):
         def E_PE(u, k):
             v = WIDE - UNIT * k
             bank["e", u] = psum.tile([P, 512], F32, name="ps")
-            nc.tensor.matmul(out=bank["e", u][:, 0:v], lhsT=ident[:], rhs=kf[u][:, 0:v], start=True, stop=False)
+            nc.tensor.matmul(out=bank["e", u][:, 0:v], lhsT=small_ident[:], rhs=ti[u][:, 0:v].bitcast(F32), start=True, stop=False)
+            nc.tensor.matmul(out=bank["e", u][:, 0:v], lhsT=big_ident[:], rhs=ones[:, 0:v], start=False, stop=False)
             nc.tensor.matmul(out=bank["e", u][:, 0:v], lhsT=neg_ident[:], rhs=acc[u][:, 0:v], start=False, stop=True)
 
         def sine_pair(u, k):
@@ -215,7 +222,7 @@ def tile_sinelayer_loe_pa_kernel(tc, in_feats, tile_gate, W, out):
             rd(p, 1, 0)
             if p + 2 < PAIRS:
                 q_x(p + 2)
-            C_ALL(p - 1); E_G(p - 1, k1)
+            C_G(p - 1, k1); E_G(p - 1, k1)
             rd(p, 1, 1)
             if p + 1 < PAIRS:
                 mm2(p + 1, 0); rd(p + 1, 0, 0, "s")
@@ -224,8 +231,10 @@ def tile_sinelayer_loe_pa_kernel(tc, in_feats, tile_gate, W, out):
             if p >= 2: sine_pair(p - 2, k2)
             if p + 1 < PAIRS:
                 rd(p + 1, 0, 1, "s")
-            if p + 3 < PAIRS:
-                tx(p + 3)
+            if p == 1:
+                tx(4)
+            if p + 4 < PAIRS:
+                tx(p + 4)
             rd(p, 2, 1)
             mm2(p, 3)
             rd(p, 3, 0); d_s(p, 0)

@@ -242,13 +242,25 @@ def tile_sinelayer_loe_pa_kernel(tc, in_feats, tile_gate, W, out):
                 rd(p, 3, 1)
         for p in range(1, PAIRS - 1):
             period(p)
+        def e_pe(u, lo, hi):
+            bank["e", u, lo] = psum.tile([P, 512], F32, name="ps")
+            o = bank["e", u, lo][:, 0:hi - lo]
+            nc.tensor.matmul(out=o, lhsT=small_ident[:], rhs=ti[u][:, lo:hi].bitcast(F32), start=True, stop=False)
+            nc.tensor.matmul(out=o, lhsT=big_ident[:], rhs=ones[:, 0:hi - lo], start=False, stop=False)
+            nc.tensor.matmul(out=o, lhsT=neg_ident[:], rhs=acc[u][:, lo:hi], start=False, stop=True)
+
+        def sine_ps(u, lo, hi):
+            nc.scalar.activation(out=get(res, u, "res", F32, 4)[:, lo:hi], in_=bank["e", u, lo][:, 0:hi - lo], func=ACT.Sin, scale=-2.0 * math.pi / STEP)
+            nc.sync.dma_start(out=o_flat[:, WIDE * u + lo:WIDE * u + hi], in_=res[u][:, lo:hi])
+
         p = PAIRS - 1
         H = COUT // 2
-        mm2(p, 1); E_PE(p - 2, K[p - 2]); d_s(p - 1, 1); rd(p, 1, 0); E_V(p - 1, K[p - 1]); C_G(p - 1, K[p - 1]); E_G(p - 1, K[p - 1])
-        mm2(p, 2); sine_pair(p - 2, K[p - 2]); rd(p, 2, 0); mm2(p, 3); rd(p, 3, 0); SIN_V(p - 1, K[p - 1]); d_s(p, 0)
+        V6 = WIDE - UNIT * K[p - 1]
+        mm2(p, 1); E_PE(p - 2, K[p - 2]); d_s(p - 1, 1); rd(p, 1, 0); C_G(p - 1, K[p - 1]); E_G(p - 1, K[p - 1])
+        mm2(p, 2); mm2(p, 3); e_pe(p - 1, 0, V6); sine_pair(p - 2, K[p - 2]); rd(p, 2, 0); rd(p, 3, 0); d_s(p, 0)
         G7 = COUT - UNIT * K[p]
         cvt_g(p, G7, COUT); sub_g(p, G7, COUT)
-        rd(p, 1, 1); rd(p, 2, 1); sub_v(p, 0, G7); SIN_G(p - 1, K[p - 1]); sine(p, 0, G7)
+        rd(p, 1, 1); sine_ps(p - 1, 0, V6); rd(p, 2, 1); sub_v(p, 0, G7); SIN_G(p - 1, K[p - 1]); sine(p, 0, G7)
         rd_part(p, 3, 1, 0, H); rd_part(p, 3, 1, H, COUT)
         round_v(p, COUT, COUT + H); round_v(p, COUT + H, WIDE)
         sub_v(p, COUT, COUT + H); sub_v(p, COUT + H, WIDE)

@@ -196,7 +196,8 @@ def tile_sinelayer_loe_pa_kernel(tc, in_feats, tile_gate, W, out):
         def rd2(u, t, eng="v"):
             rd(u, t, 0, eng); rd(u, t, 1, eng)
 
-        K = [13] * 6 + [9, 3]
+        K = [13] * 6 + [8, 3]
+        PE7 = 256
         load_x(0)
         for t in range(EXPERTS):
             load_w(t, 0); load_w(t, 1)
@@ -259,8 +260,9 @@ def tile_sinelayer_loe_pa_kernel(tc, in_feats, tile_gate, W, out):
         mm2(p, 1); E_PE(p - 2, K[p - 2]); d_s(p - 1, 1); rd(p, 1, 0); C_G(p - 1, K[p - 1]); E_G(p - 1, K[p - 1])
         mm2(p, 2); mm2(p, 3); e_pe(p - 1, 0, V6); sine_pair(p - 2, K[p - 2]); rd(p, 2, 0); rd(p, 3, 0); d_s(p, 0)
         G7 = COUT - UNIT * K[p]
-        cvt_g(p, G7, COUT); sub_g(p, G7, COUT)
-        rd(p, 1, 1); sine_ps(p - 1, 0, V6); rd(p, 2, 1); sub_v(p, 0, G7); SIN_G(p - 1, K[p - 1]); sine(p, 0, G7)
+        X7 = G7 - PE7
+        cvt_g(p, G7, COUT); sub_g(p, G7, COUT); e_pe(p, X7, G7)
+        rd(p, 1, 1); sine_ps(p - 1, 0, V6); rd(p, 2, 1); sub_v(p, 0, X7); SIN_G(p - 1, K[p - 1]); sine(p, 0, X7); sine_ps(p, X7, G7)
         rd_part(p, 3, 1, 0, H); rd_part(p, 3, 1, H, COUT)
         round_v(p, COUT, COUT + H); round_v(p, COUT + H, WIDE)
         sub_v(p, COUT, COUT + H); sub_v(p, COUT + H, WIDE)

import math
from contextlib import ExitStack

import concourse.mybir as mybir
from concourse.masks import make_identity

ROWS, CIN, COUT, EXPERTS = 2048, 512, 512, 4
FLOPS = 2 * ROWS * CIN * COUT * EXPERTS

F32 = mybir.dt.float32
BF16 = mybir.dt.bfloat16
U32 = mybir.dt.uint32
I32 = mybir.dt.int32
U8 = mybir.dt.uint8
E5M2 = mybir.dt.float8_e5m2_x4
E4M3 = mybir.dt.float8_e4m3fn_x4
ALU = mybir.AluOpType
ACT = mybir.ActivationFunctionType

P = 128
TILES = ROWS // P
PAIRS = TILES // 2
STEP = 128.0
BIAS = 1614807040.0
FBIAS = 1.5 * 2.0 ** 65
TURNS = STEP * 30.0 / (2.0 * math.pi)


def tile_sinelayer_loe_pa_kernel(tc, in_feats, tile_gate, W, out):
    nc = tc.nc
    x_hbm = in_feats.rearrange("(p n) k -> p n k", n=TILES)
    g_hbm = tile_gate.rearrange("(p n) e -> p (n e)", n=TILES)
    o_hbm = out.rearrange("(p n) c -> p n c", n=TILES)

    with ExitStack() as ctx:
        keep = ctx.enter_context(tc.tile_pool(name="keep", bufs=1))
        ring = ctx.enter_context(tc.tile_pool(name="ring", bufs=4))
        psum = ctx.enter_context(tc.psum_pool(name="psum", bufs=8))
        ctx.enter_context(tc.manual_schedule())

        g_raw = keep.tile([P, TILES * EXPERTS], BF16, name="g_raw")
        nc.scalar.dma_start(out=g_raw[:], in_=g_hbm)
        warm = keep.tile([P, 1], F32, name="warm")
        nc.vector.memset(warm[:], 0.0)
        nc.scalar.activation(out=warm[:], in_=warm[:], func=ACT.Sin)
        ident = keep.tile([P, P], F32, name="ident")
        make_identity(nc, ident[:])
        g32 = keep.tile([P, TILES * EXPERTS], F32, name="g32")
        neg_ident = keep.tile([P, P], F32, name="neg_ident")
        nc.gpsimd.tensor_scalar(out=neg_ident[:], in0=ident[:], scalar1=-1.0, scalar2=0.0, op0=ALU.mult, op1=ALU.add)
        small_ident = keep.tile([P, P], F32, name="small_ident")
        nc.gpsimd.tensor_scalar(out=small_ident[:], in0=ident[:], scalar1=2.0 ** -42, scalar2=0.0, op0=ALU.mult, op1=ALU.add)
        big_ident = keep.tile([P, P], BF16, name="big_ident")
        nc.gpsimd.tensor_scalar(out=big_ident[:], in0=ident[:], scalar1=-1.5 * 2.0 ** 23, scalar2=0.0, op0=ALU.mult, op1=ALU.add)
        ones = keep.tile([P, 512], BF16, name="ones")
        nc.gpsimd.memset(ones[:], 1.0)

        x_raw, w_raw = {}, {}

        def load_x(u):
            x_raw[u] = keep.tile([P, 2, CIN], BF16, name="x_raw%d" % u)
            nc.sync.dma_start(out=x_raw[u][:], in_=x_hbm[:, 2 * u:2 * u + 2, :])

        def load_w(t, b):
            w_raw[t, b] = keep.tile([P, 2, CIN], BF16, name="w_raw%d_%d" % (t, b))
            nc.sync.dma_start(out=w_raw[t, b][:], in_=W[t].rearrange("(p j) k -> p j k", j=4)[:, 2 * b:2 * b + 2, :])

        bank = {}

        def transposes(key, raw):
            bank[key] = psum.tile([P, 512], F32, name="ps")
            words = raw[:].rearrange("p s k -> p (s k)").bitcast(F32)
            for s in range(2):
                for e in range(2):
                    nc.tensor.transpose(bank[key][:, (2 * s + e) * P:(2 * s + e + 1) * P],
                                        words[:, 256 * s + e:256 * (s + 1):2], ident[:])

        def copy_on(eng, dst, src):
            if eng == "v":
                nc.vector.tensor_copy(out=dst, in_=src)
            else:
                nc.scalar.copy(out=dst, in_=src)

        xg, xc, xs, wg, wc, ws = {}, {}, {}, {}, {}, {}

        def a_x(u, eng):
            xg[u] = keep.tile([P, 1024], BF16, name="xg%d" % u, align_bytes=64)
            copy_on(eng, xg[u][:].bitcast(F32).rearrange("q (s m e) -> q s m e", s=2, e=2),
                    bank["x", u][:].rearrange("q (s e m) -> q s m e", s=2, e=2))

        def q_x(u):
            xc[u] = keep.tile([P, 256], U32, name="xc%d" % u, align_bytes=64)
            xs[u] = keep.tile([P, 256], U8, name="xs%d" % u, align_bytes=64)
            nc.vector.quantize_mx(out=xc[u][:].bitcast(E5M2), scales=xs[u][:], in_=xg[u][:])

        def a_w(t, b, eng):
            if b == 0:
                wg[t] = keep.tile([P, 2048], BF16, name="wg%d" % t, align_bytes=64)
            copy_on(eng, wg[t][:].bitcast(F32).rearrange("q (m b r) -> q m b r", b=2, r=4)[:, :, b, :],
                    bank["w", t, b][:].rearrange("q (r m) -> q m r", r=4))

        def q_w(t):
            wc[t] = keep.tile([P, 512], U32, name="wc%d" % t, align_bytes=64)
            ws[t] = keep.tile([P, 512], U8, name="ws%d" % t, align_bytes=64)
            nc.vector.quantize_mx(out=wc[t][:].bitcast(E4M3), scales=ws[t][:], in_=wg[t][:])

        def mm(u, t, s):
            bank[u, t, s] = psum.tile([P, 512], F32, name="ps")
            cols = slice(P * s, P * (s + 1))
            nc.tensor.matmul_mx(out=bank[u, t, s][:], lhsT=xc[u][:, cols].bitcast(E5M2), lhsT_scale=xs[u][:, cols],
                                rhs=wc[t][:].bitcast(E4M3), rhs_scale=ws[t][:], start=True, stop=True)

        acc, ti, kf, fr, res = {}, {}, {}, {}, {}
        UNIT = 64
        WIDE = 2 * COUT
        o_flat = out.rearrange("(p n) c -> p (n c)", n=TILES)

        def gcol(u, t, s):
            c = (2 * u + s) * EXPERTS + t
            return g32[:, c:c + 1]

        def get(d, u, name, dt, bufs):
            if u not in d:
                d[u] = ring.tile([P, WIDE], dt, name=name, bufs=bufs)
            return d[u]

        def rd_part(u, t, s, lo, hi):
            a = acc[u][:, COUT * s + lo:COUT * s + hi]
            nc.vector.scalar_tensor_tensor(out=a, in0=bank[u, t, s][:, lo:hi], scalar=gcol(u, t, s), in1=a, op0=ALU.mult, op1=ALU.add)

        def rd(u, t, s, eng="v"):
            a = get(acc, u, "acc", F32, 6)[:, COUT * s:COUT * (s + 1)]
            if t == 0 and eng == "s":
                nc.scalar.activation(out=a, in_=bank[u, 0, s][:], func=ACT.Copy, scale=gcol(u, 0, s))
            elif t == 0:
                nc.vector.tensor_scalar(out=a, in0=bank[u, 0, s][:], scalar1=gcol(u, 0, s), scalar2=None, op0=ALU.mult)
            else:
                nc.vector.scalar_tensor_tensor(out=a, in0=bank[u, t, s][:], scalar=gcol(u, t, s), in1=a, op0=ALU.mult, op1=ALU.add)

        def round_s(u, lo, hi):
            nc.scalar.activation(out=get(ti, u, "ti", I32, 4)[:, lo:hi].bitcast(U32), in_=acc[u][:, lo:hi], func=ACT.Copy,
                                 bias=BIAS, scale=1.0)

        def round_v(u, lo, hi):
            nc.vector.tensor_scalar(out=get(ti, u, "ti", I32, 4)[:, lo:hi], in0=acc[u][:, lo:hi], scalar1=BIAS, scalar2=None, op0=ALU.add)

        def cvt_g(u, lo, hi):
            nc.gpsimd.tensor_scalar(out=get(kf, u, "kf", F32, 4)[:, lo:hi], in0=ti[u][:, lo:hi].bitcast(F32), scalar1=-FBIAS,
                                    scalar2=2.0 ** -42, op0=ALU.add, op1=ALU.mult)

        def sub_g(u, lo, hi):
            nc.gpsimd.tensor_tensor(out=get(fr, u, "fr", F32, 4)[:, lo:hi], in0=kf[u][:, lo:hi], in1=acc[u][:, lo:hi],
                                    op=ALU.subtract)

        def sub_v(u, lo, hi):
            nc.vector.scalar_tensor_tensor(out=get(fr, u, "fr", F32, 4)[:, lo:hi], in0=ti[u][:, lo:hi], scalar=BIAS,
                                           in1=acc[u][:, lo:hi], op0=ALU.subtract, op1=ALU.subtract)

        def sine(u, lo, hi):
            nc.scalar.activation(out=get(res, u, "res", F32, 4)[:, lo:hi], in_=fr[u][:, lo:hi], func=ACT.Sin, scale=-2.0 * math.pi / STEP)
            nc.sync.dma_start(out=o_flat[:, WIDE * u + lo:WIDE * u + hi], in_=res[u][:, lo:hi])

        def C_G(u, k): cvt_g(u, WIDE - UNIT * k, WIDE)

        def C_ALL(u): cvt_g(u, 0, WIDE)

        def E_PE(u, k):
            v = WIDE - UNIT * k
            bank["e", u] = psum.tile([P, 512], F32, name="ps")
            nc.tensor.matmul(out=bank["e", u][:, 0:v], lhsT=small_ident[:], rhs=ti[u][:, 0:v].bitcast(F32), start=True, stop=False)
            nc.tensor.matmul(out=bank["e", u][:, 0:v], lhsT=big_ident[:], rhs=ones[:, 0:v], start=False, stop=False)
            nc.tensor.matmul(out=bank["e", u][:, 0:v], lhsT=neg_ident[:], rhs=acc[u][:, 0:v], start=False, stop=True)

        def sine_pair(u, k):
            v = WIDE - UNIT * k
            nc.scalar.activation(out=get(res, u, "res", F32, 4)[:, 0:v], in_=bank["e", u][:, 0:v], func=ACT.Sin, scale=-2.0 * math.pi / STEP)
            nc.scalar.activation(out=res[u][:, v:WIDE], in_=fr[u][:, v:WIDE], func=ACT.Sin, scale=-2.0 * math.pi / STEP)
            nc.sync.dma_start(out=o_flat[:, WIDE * u:WIDE * (u + 1)], in_=res[u][:])
        def E_G(u, k): sub_g(u, WIDE - UNIT * k, WIDE)
        def E_V(u, k): sub_v(u, 0, WIDE - UNIT * k)
        def SIN_G(u, k): sine(u, WIDE - UNIT * k, WIDE)
        def SIN_V(u, k): sine(u, 0, WIDE - UNIT * k)
        def d_s(u, s): round_s(u, COUT * s, COUT * (s + 1))
        def e_v(u, s): sub_v(u, COUT * s, COUT * (s + 1))
        def f_(u, s): sine(u, COUT * s, COUT * (s + 1))

        def tx(u, eng="s"):
            transposes(("x", u), x_raw[u]); a_x(u, eng)

        def tw(t, b, eng="s"):
            transposes(("w", t, b), w_raw[t, b]); a_w(t, b, eng)

        def mm2(u, t):
            mm(u, t, 0); mm(u, t, 1)

        def rd2(u, t, eng="v"):
            rd(u, t, 0, eng); rd(u, t, 1, eng)

        K = [13] * 6 + [8, 3]
        PE7 = 256
        load_x(0)
        for t in range(EXPERTS):
            load_w(t, 0); load_w(t, 1)
        for u in range(1, PAIRS):
            load_x(u)
        nc.vector.tensor_scalar(out=g32[:], in0=g_raw[:], scalar1=TURNS, scalar2=None, op0=ALU.mult)

        tx(0, "v"); q_x(0); tw(0, 0); tw(0, 1, "v"); q_w(0)
        tw(1, 0); tw(1, 1); tw(2, 0, "v"); q_w(1)
        tw(2, 1); mm2(0, 0); rd(0, 0, 0, "s"); rd(0, 0, 1, "v"); tw(3, 0); q_w(2); tw(3, 1)
        mm2(0, 1); rd2(0, 1)
        tx(1); q_w(3)
        mm2(0, 2); q_x(1); rd2(0, 2)
        tx(2); tx(3); q_x(2)
        mm2(0, 3); mm2(1, 0); rd(0, 3, 0); rd(0, 3, 1)
        rd2(1, 0, "s"); d_s(0, 0)

        def period(p):
            k1 = K[p - 1]; k2 = K[p - 2] if p >= 2 else 0
            mm2(p, 1)
            if p >= 2: E_PE(p - 2, k2)
            d_s(p - 1, 1)
            rd(p, 1, 0)
            if p + 2 < PAIRS:
                q_x(p + 2)
            C_G(p - 1, k1); E_G(p - 1, k1)
            rd(p, 1, 1)
            if p + 1 < PAIRS:
                mm2(p + 1, 0); rd(p + 1, 0, 0, "s")
            mm2(p, 2)
            rd(p, 2, 0)
            if p >= 2: sine_pair(p - 2, k2)
            if p + 1 < PAIRS:
                rd(p + 1, 0, 1, "s")
            if p == 1:
                tx(4)
            if p + 4 < PAIRS:
                tx(p + 4)
            rd(p, 2, 1)
            mm2(p, 3)
            rd(p, 3, 0); d_s(p, 0)
            if p < PAIRS - 1:
                rd(p, 3, 1)
        for p in range(1, PAIRS - 1):
            period(p)
        def e_pe(u, lo, hi):
            bank["e", u, lo] = psum.tile([P, 512], F32, name="ps")
            o = bank["e", u, lo][:, 0:hi - lo]
            nc.tensor.matmul(out=o, lhsT=small_ident[:], rhs=ti[u][:, lo:hi].bitcast(F32), start=True, stop=False)
            nc.tensor.matmul(out=o, lhsT=big_ident[:], rhs=ones[:, 0:hi - lo], start=False, stop=False)
            nc.tensor.matmul(out=o, lhsT=neg_ident[:], rhs=acc[u][:, lo:hi], start=False, stop=True)

        def sine_ps(u, lo, hi):
            nc.scalar.activation(out=get(res, u, "res", F32, 4)[:, lo:hi], in_=bank["e", u, lo][:, 0:hi - lo], func=ACT.Sin, scale=-2.0 * math.pi / STEP)
            nc.sync.dma_start(out=o_flat[:, WIDE * u + lo:WIDE * u + hi], in_=res[u][:, lo:hi])

        p = PAIRS - 1
        H = COUT // 2
        V6 = WIDE - UNIT * K[p - 1]
        mm2(p, 1); E_PE(p - 2, K[p - 2]); d_s(p - 1, 1); rd(p, 1, 0); C_G(p - 1, K[p - 1]); E_G(p - 1, K[p - 1])
        mm2(p, 2); mm2(p, 3); e_pe(p - 1, 0, V6); sine_pair(p - 2, K[p - 2]); rd(p, 2, 0); rd(p, 3, 0); d_s(p, 0)
        G7 = COUT - UNIT * K[p]
        X7 = G7 - PE7
        cvt_g(p, G7, COUT); sub_g(p, G7, COUT); e_pe(p, X7, G7)
        rd(p, 1, 1); sine_ps(p - 1, 0, V6); rd(p, 2, 1); sub_v(p, 0, X7); SIN_G(p - 1, K[p - 1]); sine(p, 0, X7); sine_ps(p, X7, G7)
        rd_part(p, 3, 1, 0, H); rd_part(p, 3, 1, H, COUT)
        round_v(p, COUT, COUT + H); round_v(p, COUT + H, WIDE)
        sub_v(p, COUT, COUT + H); sub_v(p, COUT + H, WIDE)
        sine(p, G7, COUT); sine(p, COUT, COUT + H); sine(p, COUT + H, WIDE)
